import numpy as np
import ml_dtypes


def mxq(x, axis, fmt="e4m3"):
    dtype, down = {"e4m3": (ml_dtypes.float8_e4m3fn, 7), "e5m2": (ml_dtypes.float8_e5m2, 14)}[fmt]
    v = np.moveaxis(np.asarray(x, np.float32).astype(ml_dtypes.bfloat16).astype(np.float64), axis, -1)
    blocks = v.reshape(v.shape[:-1] + (-1, 32))
    amax = np.abs(blocks).max(-1, keepdims=True)
    byte = np.maximum(np.where(amax > 0, np.frexp(amax)[1] - 1 + 127, 0) - down, 1)
    scale = np.exp2(byte - 127.0)
    codes = (blocks / scale).astype(np.float32).astype(dtype).astype(np.float64)
    return np.moveaxis((codes * scale).reshape(v.shape), -1, axis)


WIDE = False


def mx_kscale(k):
    if not WIDE:
        return np.ones(k)
    levels = np.array([10, -10, 5, -5, 0])
    a = np.random.permutation(np.resize(levels, k // 512 * 4)).reshape(k // 512, 4)
    idx = np.arange(k)
    return np.exp2(a[idx // 512, idx % 128 // 32])


BF16 = ml_dtypes.bfloat16


def bf(x):
    return np.asarray(x, np.float32).astype(BF16)


def f64(x):
    return np.asarray(x).astype(np.float64)


B, S, M, D, H = 32, 128, 3, 512, 512


def setup_inputs():
    s = mx_kscale(2 * D)
    lens = np.random.randint(0, M + 1, (B, S))
    valid = (np.arange(M)[None, None, :] < lens[:, :, None]).astype(np.float64)
    src = np.random.standard_normal((B, S, M, D)) / np.sqrt(M) * s[:D]
    neigh = np.random.standard_normal((B, S, M, D)) * 2.0 * valid[..., None] * s[D:]
    return {"src_node_features": bf(src), "neigh_node_features": bf(neigh),
            "W_map": bf(np.random.standard_normal((2 * D, H)) / np.sqrt(2 * D) / s[:, None]),
            "b_map": bf(-0.5 + 0.3 * np.random.standard_normal(H))}


def reference(src_node_features, neigh_node_features, W_map, b_map):
    src, neigh = f64(src_node_features), f64(neigh_node_features)
    valid = np.any(neigh != 0, axis=-1)
    num = np.sum(valid, axis=-1).astype(np.float64)
    neigh_mean = neigh.sum(axis=2) / np.maximum(num, 1.0)[..., None]
    hidden = np.concatenate([src.sum(axis=2), neigh_mean], axis=-1)
    hidden = hidden.reshape(-1, hidden.shape[-1])
    v = (mxq(hidden, 1, "e4m3") @ mxq(f64(W_map), 0, "e4m3")) + f64(b_map)
    return np.where(v >= 0, v, 0.01 * v)

@@ -1,0 +1,205 @@
+import concourse.mybir as mybir
+from concourse.masks import make_identity
+
+F32 = mybir.dt.float32
+BF16 = mybir.dt.bfloat16
+U32 = mybir.dt.uint32
+U8 = mybir.dt.uint8
+FP8X4 = mybir.dt.float8_e4m3fn_x4
+ALU = mybir.AluOpType
+ACT = mybir.ActivationFunctionType
+AXIS = mybir.AxisListType
+
+P = 128
+SLOTS = 3
+D = 512
+H = 512
+K = 2 * D
+NODES = 4096
+K_PASS = 512
+PASSES = K // K_PASS
+NODE_TILES = NODES // P
+PAIR = 2
+N_PAIRS = NODE_TILES // PAIR
+PREFETCH = 3
+SLOPE = 0.01
+
+FLOPS = 2 * NODES * K * H
+
+
+def tile_syntacticgcn_t_kernel(tc, src_node_features, neigh_node_features, W_map, b_map, out):
+    nc = tc.nc
+
+    src_v = src_node_features.rearrange("b (q t) m d -> (b q) t (m d)", t=NODE_TILES)
+    neigh_v = neigh_node_features.rearrange("b (q t) m d -> (b q) t (m d)", t=NODE_TILES)
+    out_v = out.rearrange("(p t) h -> p t h", t=NODE_TILES)
+
+    with tc.tile_pool(name="const", bufs=1) as const, tc.tile_pool(name="data", bufs=PREFETCH + 1) as data, tc.tile_pool(
+        name="work", bufs=2
+    ) as work, tc.tile_pool(name="junk", bufs=4) as junk_pool, tc.psum_pool(name="psum", bufs=4) as psum:
+        w_raw = const.tile([P, PASSES * 4 * H], BF16)
+        nc.sync.dma_start(
+            out=w_raw[:].rearrange("p (c eh) -> p c eh", c=2 * PASSES),
+            in_=W_map.rearrange("(c q e) h -> q c (e h)", c=2 * PASSES, e=2),
+        )
+        ident = const.tile([P, P], F32)
+        make_identity(nc, ident[:])
+
+        xs_of = {}
+        xn_of = {}
+
+        def load(c):
+            xn = data.tile([P, PAIR, SLOTS * D], BF16)
+            nc.sync.dma_start(out=xn[:], in_=neigh_v[:, PAIR * c : PAIR * (c + 1), :])
+            xs = data.tile([P, PAIR, SLOTS * D], BF16)
+            nc.sync.dma_start(out=xs[:], in_=src_v[:, PAIR * c : PAIR * (c + 1), :])
+            xn_of[c] = xn
+            xs_of[c] = xs
+
+        for c in range(PREFETCH):
+            load(c)
+        bias_bf = const.tile([P, H], BF16)
+        nc.sync.dma_start(out=bias_bf[:], in_=b_map.partition_broadcast(P))
+
+        w_grouped = const.tile([P, PASSES * H * 4], BF16, align_bytes=64)
+        w_codes = const.tile([P, PASSES * H], U32, align_bytes=64)
+        w_scales = const.tile([P, PASSES * H], U8, align_bytes=64)
+        for g in range(PASSES):
+            nc.vector.tensor_copy(
+                out=w_grouped[:, g * 4 * H : (g + 1) * 4 * H].rearrange("p (h t) -> p h t", t=4),
+                in_=w_raw[:, g * 4 * H : (g + 1) * 4 * H].rearrange("p (t h) -> p h t", t=4),
+            )
+        for g in range(PASSES):
+            nc.vector.quantize_mx(
+                out=w_codes[:, g * H : (g + 1) * H].bitcast(FP8X4),
+                scales=w_scales[:, g * H : (g + 1) * H],
+                in_=w_grouped[:, g * 4 * H : (g + 1) * 4 * H],
+            )
+        bias = const.tile([P, H], F32)
+        nc.vector.tensor_copy(out=bias[:], in_=bias_bf[:])
+
+        abs_sum_of = {}
+        recip_of = {}
+        hid_of = {}
+        nsum_of = {}
+        xt_of = {}
+        grouped_of = {}
+        acc_of = {}
+
+        def count(c):
+            abs_sum = work.tile([P, PAIR * SLOTS], F32)
+            for j in range(PAIR):
+                for s in range(SLOTS):
+                    junk = junk_pool.tile([P, D], BF16)
+                    nc.scalar.activation(
+                        out=junk[:],
+                        in_=xn_of[c][:, j, s * D : (s + 1) * D],
+                        func=ACT.Abs,
+                        accum_out=abs_sum[:, j * SLOTS + s : j * SLOTS + s + 1],
+                    )
+            abs_sum_of[c] = abs_sum
+
+        def reciprocal_count(c):
+            valid = work.tile([P, PAIR, SLOTS], F32)
+            nc.vector.tensor_scalar(
+                out=valid[:].rearrange("p j s -> p (j s)"), in0=abs_sum_of[c][:], scalar1=0.0, scalar2=None, op0=ALU.is_gt
+            )
+            num = work.tile([P, PAIR], F32)
+            nc.vector.tensor_reduce(out=num[:], in_=valid[:], axis=AXIS.X, op=ALU.add)
+            den = work.tile([P, PAIR], F32)
+            nc.vector.tensor_scalar_max(den[:], num[:], 1.0)
+            recip = work.tile([P, PAIR], F32)
+            nc.vector.reciprocal(recip[:], den[:])
+            recip_of[c] = recip
+
+        def sums(c):
+            xs = xs_of[c]
+            xn = xn_of[c]
+            hid = work.tile([P, PAIR, K], BF16)
+            s01 = work.tile([P, PAIR, D], F32)
+            n01 = work.tile([P, PAIR, D], F32)
+            nsum = work.tile([P, PAIR, D], F32)
+            nc.vector.tensor_tensor(out=s01[:], in0=xs[:, :, 0:D], in1=xs[:, :, D : 2 * D], op=ALU.add)
+            nc.vector.tensor_tensor(out=n01[:], in0=xn[:, :, 0:D], in1=xn[:, :, D : 2 * D], op=ALU.add)
+            nc.vector.tensor_tensor(out=hid[:, :, 0:D], in0=s01[:], in1=xs[:, :, 2 * D : 3 * D], op=ALU.add)
+            nc.vector.tensor_tensor(out=nsum[:], in0=n01[:], in1=xn[:, :, 2 * D : 3 * D], op=ALU.add)
+            hid_of[c] = hid
+            nsum_of[c] = nsum
+
+        def scale(c):
+            for j in range(PAIR):
+                nc.scalar.activation(
+                    out=hid_of[c][:, j, D:K], in_=nsum_of[c][:, j, :], func=ACT.Copy, scale=recip_of[c][:, j : j + 1]
+                )
+
+        def transpose(c):
+            words = hid_of[c][:].rearrange("p j k -> p (j k)").bitcast(F32)
+            xts = []
+            for j in range(PAIR):
+                xt = psum.tile([P, 2 * PASSES, P], F32)
+                for cu in range(2 * PASSES):
+                    first = j * (K // 2) + cu * P
+                    nc.tensor.transpose(xt[:, cu, :], words[:, first : first + P], ident[:])
+                xts.append(xt)
+            xt_of[c] = xts
+
+        def regroup(c):
+            grouped = work.tile([P, PAIR * K], BF16, align_bytes=64)
+            grouped_w = grouped[:].bitcast(F32).rearrange("p (j g n u) -> p j g n u", j=PAIR, g=PASSES, u=2)
+            for j in range(PAIR):
+                nc.scalar.copy(out=grouped_w[:, j], in_=xt_of[c][j][:].rearrange("p (g u) n -> p g n u", u=2))
+            grouped_of[c] = grouped
+
+        def quantise_and_multiply(c):
+            codes = work.tile([P, PAIR * PASSES * P], U32, align_bytes=64)
+            scales = work.tile([P, PAIR * PASSES * P], U8, align_bytes=64)
+            nc.vector.quantize_mx(out=codes[:].bitcast(FP8X4), scales=scales[:], in_=grouped_of[c][:])
+            accs = []
+            for j in range(PAIR):
+                acc = psum.tile([P, H], F32)
+                for g in range(PASSES):
+                    cols = slice((j * PASSES + g) * P, (j * PASSES + g + 1) * P)
+                    nc.tensor.matmul_mx(
+                        out=acc[:],
+                        lhsT=codes[:, cols].bitcast(FP8X4),
+                        lhsT_scale=scales[:, cols],
+                        rhs=w_codes[:, g * H : (g + 1) * H].bitcast(FP8X4),
+                        rhs_scale=w_scales[:, g * H : (g + 1) * H],
+                        start=(g == 0),
+                        stop=(g == PASSES - 1),
+                    )
+                accs.append(acc)
+            acc_of[c] = accs
+
+        def finish(c):
+            biased = work.tile([P, PAIR, H], F32)
+            result = work.tile([P, PAIR, H], F32)
+            for j in range(PAIR):
+                nc.vector.tensor_tensor(out=biased[:, j, :], in0=acc_of[c][j][:], in1=bias[:], op=ALU.add)
+            for j in range(PAIR):
+                nc.vector.scalar_tensor_tensor(
+                    out=result[:, j, :], in0=biased[:, j, :], scalar=SLOPE, in1=biased[:, j, :], op0=ALU.mult, op1=ALU.max
+                )
+            nc.sync.dma_start(out=out_v[:, PAIR * c : PAIR * (c + 1), :], in_=result[:])
+
+        count(0)
+        reciprocal_count(0)
+        for i in range(N_PAIRS + 2):
+            if i + PREFETCH < N_PAIRS:
+                load(i + PREFETCH)
+            if i + 1 < N_PAIRS:
+                count(i + 1)
+            if i < N_PAIRS:
+                sums(i)
+            if i + 1 < N_PAIRS:
+                reciprocal_count(i + 1)
+            if 0 <= i - 1 < N_PAIRS:
+                regroup(i - 1)
+            if i < N_PAIRS:
+                scale(i)
+            if 0 <= i - 2:
+                finish(i - 2)
+            if 0 <= i - 1 < N_PAIRS:
+                quantise_and_multiply(i - 1)
+            if i < N_PAIRS:
+                transpose(i)

@@ -36,7 +36,7 @@ def tile_syntacticgcn_t_kernel(tc, src_node_features, neigh_node_features, W_map
 
     with tc.tile_pool(name="const", bufs=1) as const, tc.tile_pool(name="data", bufs=PREFETCH + 1) as data, tc.tile_pool(
         name="work", bufs=2
-    ) as work, tc.tile_pool(name="junk", bufs=4) as junk_pool, tc.psum_pool(name="psum", bufs=4) as psum:
+    ) as work, tc.tile_pool(name="junk", bufs=4) as junk_pool, tc.psum_pool(name="psum", bufs=1) as psum:
         w_raw = const.tile([P, PASSES * 4 * H], BF16)
         nc.sync.dma_start(
             out=w_raw[:].rearrange("p (c eh) -> p c eh", c=2 * PASSES),
@@ -80,9 +80,12 @@ def tile_syntacticgcn_t_kernel(tc, src_node_features, neigh_node_features, W_map
 
         abs_sum_of = {}
         recip_of = {}
-        hid_of = {}
+        n01_of = {}
         nsum_of = {}
-        xt_of = {}
+        mean_of = {}
+        src_t_of = {}
+        first_of = {}
+        mean_t_of = {}
         grouped_of = {}
         acc_of = {}
 
@@ -112,43 +115,69 @@ def tile_syntacticgcn_t_kernel(tc, src_node_features, neigh_node_features, W_map
             nc.vector.reciprocal(recip[:], den[:])
             recip_of[c] = recip
 
-        def sums(c):
-            xs = xs_of[c]
+        def add_first_two_neigh_slots(c):
             xn = xn_of[c]
-            hid = work.tile([P, PAIR, K], BF16)
-            s01 = work.tile([P, PAIR, D], F32)
             n01 = work.tile([P, PAIR, D], F32)
+            nc.gpsimd.tensor_tensor(out=n01[:], in0=xn[:, :, 0:D], in1=xn[:, :, D : 2 * D], op=ALU.add)
+            n01_of[c] = n01
+
+        def transpose_src(c):
+            words = xs_of[c][:].rearrange("p j f -> p (j f)").bitcast(F32)
+            banks = []
+            for s in range(SLOTS):
+                bank = psum.tile([P, PAIR, 2, P], F32, tag="src_t%d" % s, name="src_t%d" % s)
+                for j in range(PAIR):
+                    for u in range(2):
+                        first = (j * SLOTS + s) * (D // 2) + u * P
+                        nc.tensor.transpose(bank[:, j, u, :], words[:, first : first + P], ident[:])
+                banks.append(bank)
+            src_t_of[c] = banks
+
+        def copy_first_src_slot(c):
+            first = work.tile([P, PAIR * D // 2], F32)
+            nc.scalar.copy(out=first[:], in_=src_t_of[c][0][:].rearrange("p j u n -> p (j u n)"))
+            first_of[c] = first
+
+        def sums(c):
+            xn = xn_of[c]
+            slot1 = src_t_of[c][1][:].rearrange("p j u n -> p (j u n)").bitcast(BF16)
+            slot2 = src_t_of[c][2][:].rearrange("p j u n -> p (j u n)").bitcast(BF16)
+            s01 = work.tile([P, PAIR * D], F32)
             nsum = work.tile([P, PAIR, D], F32)
-            nc.vector.tensor_tensor(out=s01[:], in0=xs[:, :, 0:D], in1=xs[:, :, D : 2 * D], op=ALU.add)
-            nc.vector.tensor_tensor(out=n01[:], in0=xn[:, :, 0:D], in1=xn[:, :, D : 2 * D], op=ALU.add)
-            nc.vector.tensor_tensor(out=hid[:, :, 0:D], in0=s01[:], in1=xs[:, :, 2 * D : 3 * D], op=ALU.add)
-            nc.vector.tensor_tensor(out=nsum[:], in0=n01[:], in1=xn[:, :, 2 * D : 3 * D], op=ALU.add)
-            hid_of[c] = hid
+            grouped = work.tile([P, PAIR * K], BF16, align_bytes=64, bufs=3)
+            nc.vector.tensor_tensor(out=s01[:], in0=first_of[c][:].bitcast(BF16), in1=slot1, op=ALU.add)
+            nc.vector.tensor_tensor(out=nsum[:], in0=n01_of[c][:], in1=xn[:, :, 2 * D : 3 * D], op=ALU.add)
+            grouped_v = grouped[:].rearrange("p (j g n u e) -> p j g n u e", j=PAIR, g=PASSES, u=2, e=2)
+            for j in range(PAIR):
+                nc.vector.tensor_tensor(
+                    out=grouped_v[:, j, 0],
+                    in0=s01[:, j * D : (j + 1) * D].rearrange("p (u n e) -> p n u e", u=2, e=2),
+                    in1=slot2[:, j * D : (j + 1) * D].rearrange("p (u n e) -> p n u e", u=2, e=2),
+                    op=ALU.add,
+                )
             nsum_of[c] = nsum
+            grouped_of[c] = grouped
 
         def scale(c):
+            mean = work.tile([P, PAIR, D], BF16)
             for j in range(PAIR):
                 nc.scalar.activation(
-                    out=hid_of[c][:, j, D:K], in_=nsum_of[c][:, j, :], func=ACT.Copy, scale=recip_of[c][:, j : j + 1]
+                    out=mean[:, j, :], in_=nsum_of[c][:, j, :], func=ACT.Copy, scale=recip_of[c][:, j : j + 1]
                 )
+            mean_of[c] = mean
 
-        def transpose(c):
-            words = hid_of[c][:].rearrange("p j k -> p (j k)").bitcast(F32)
-            xts = []
+        def transpose_mean(c):
+            words = mean_of[c][:].rearrange("p j k -> p (j k)").bitcast(F32)
+            mean_t = psum.tile([P, PAIR, 2, P], F32)
             for j in range(PAIR):
-                xt = psum.tile([P, 2 * PASSES, P], F32)
-                for cu in range(2 * PASSES):
-                    first = j * (K // 2) + cu * P
-                    nc.tensor.transpose(xt[:, cu, :], words[:, first : first + P], ident[:])
-                xts.append(xt)
-            xt_of[c] = xts
+                for u in range(2):
+                    first = j * (D // 2) + u * P
+                    nc.tensor.transpose(mean_t[:, j, u, :], words[:, first : first + P], ident[:])
+            mean_t_of[c] = mean_t
 
-        def regroup(c):
-            grouped = work.tile([P, PAIR * K], BF16, align_bytes=64)
-            grouped_w = grouped[:].bitcast(F32).rearrange("p (j g n u) -> p j g n u", j=PAIR, g=PASSES, u=2)
-            for j in range(PAIR):
-                nc.scalar.copy(out=grouped_w[:, j], in_=xt_of[c][j][:].rearrange("p (g u) n -> p g n u", u=2))
-            grouped_of[c] = grouped
+        def regroup_mean(c):
+            grouped_w = grouped_of[c][:].bitcast(F32).rearrange("p (j g n u) -> p j g n u", j=PAIR, g=PASSES, u=2)
+            nc.scalar.copy(out=grouped_w[:, :, 1], in_=mean_t_of[c][:].rearrange("p j u n -> p j n u"))
 
         def quantise_and_multiply(c):
             codes = work.tile([P, PAIR * PASSES * P], U32, align_bytes=64)
@@ -156,7 +185,7 @@ def tile_syntacticgcn_t_kernel(tc, src_node_features, neigh_node_features, W_map
             nc.vector.quantize_mx(out=codes[:].bitcast(FP8X4), scales=scales[:], in_=grouped_of[c][:])
             accs = []
             for j in range(PAIR):
-                acc = psum.tile([P, H], F32)
+                acc = psum.tile([P, H], F32, bufs=4)
                 for g in range(PASSES):
                     cols = slice((j * PASSES + g) * P, (j * PASSES + g + 1) * P)
                     nc.tensor.matmul_mx(
@@ -184,17 +213,23 @@ def tile_syntacticgcn_t_kernel(tc, src_node_features, neigh_node_features, W_map
 
         count(0)
         reciprocal_count(0)
+        add_first_two_neigh_slots(0)
+        transpose_src(0)
+        copy_first_src_slot(0)
         for i in range(N_PAIRS + 2):
             if i + PREFETCH < N_PAIRS:
                 load(i + PREFETCH)
             if i + 1 < N_PAIRS:
+                add_first_two_neigh_slots(i + 1)
                 count(i + 1)
             if i < N_PAIRS:
                 sums(i)
             if i + 1 < N_PAIRS:
+                transpose_src(i + 1)
+                copy_first_src_slot(i + 1)
                 reciprocal_count(i + 1)
             if 0 <= i - 1 < N_PAIRS:
-                regroup(i - 1)
+                regroup_mean(i - 1)
             if i < N_PAIRS:
                 scale(i)
             if 0 <= i - 2:
@@ -202,4 +237,4 @@ def tile_syntacticgcn_t_kernel(tc, src_node_features, neigh_node_features, W_map
             if 0 <= i - 1 < N_PAIRS:
                 quantise_and_multiply(i - 1)
             if i < N_PAIRS:
-                transpose(i)
+                transpose_mean(i)

@@ -118,7 +118,7 @@ def tile_syntacticgcn_t_kernel(tc, src_node_features, neigh_node_features, W_map
         def add_first_two_neigh_slots(c):
             xn = xn_of[c]
             n01 = work.tile([P, PAIR, D], F32)
-            nc.gpsimd.tensor_tensor(out=n01[:], in0=xn[:, :, 0:D], in1=xn[:, :, D : 2 * D], op=ALU.add)
+            nc.vector.tensor_tensor(out=n01[:], in0=xn[:, :, 0:D], in1=xn[:, :, D : 2 * D], op=ALU.add)
             n01_of[c] = n01
 
         def transpose_src(c):

@@ -36,11 +36,11 @@ def tile_syntacticgcn_t_kernel(tc, src_node_features, neigh_node_features, W_map
 
     with tc.tile_pool(name="const", bufs=1) as const, tc.tile_pool(name="data", bufs=PREFETCH + 1) as data, tc.tile_pool(
         name="work", bufs=2
-    ) as work, tc.tile_pool(name="junk", bufs=4) as junk_pool, tc.psum_pool(name="psum", bufs=1) as psum:
+    ) as work, tc.tile_pool(name="junk", bufs=4) as junk_pool, tc.psum_pool(name="psum", bufs=4) as psum:
         w_raw = const.tile([P, PASSES * 4 * H], BF16)
         nc.sync.dma_start(
-            out=w_raw[:].rearrange("p (c eh) -> p c eh", c=2 * PASSES),
-            in_=W_map.rearrange("(c q e) h -> q c (e h)", c=2 * PASSES, e=2),
+            out=w_raw[:].rearrange("p (c h) -> p c h", c=4 * PASSES),
+            in_=W_map.rearrange("(c p) h -> p c h", p=P),
         )
         ident = const.tile([P, P], F32)
         make_identity(nc, ident[:])
@@ -80,12 +80,8 @@ def tile_syntacticgcn_t_kernel(tc, src_node_features, neigh_node_features, W_map
 
         abs_sum_of = {}
         recip_of = {}
-        n01_of = {}
-        nsum_of = {}
-        mean_of = {}
-        src_t_of = {}
-        first_of = {}
-        mean_t_of = {}
+        wide_of = {}
+        hid_t_of = {}
         grouped_of = {}
         acc_of = {}
 
@@ -115,69 +111,41 @@ def tile_syntacticgcn_t_kernel(tc, src_node_features, neigh_node_features, W_map
             nc.vector.reciprocal(recip[:], den[:])
             recip_of[c] = recip
 
-        def add_first_two_neigh_slots(c):
-            xn = xn_of[c]
-            n01 = work.tile([P, PAIR, D], F32)
-            nc.vector.tensor_tensor(out=n01[:], in0=xn[:, :, 0:D], in1=xn[:, :, D : 2 * D], op=ALU.add)
-            n01_of[c] = n01
+        def widen(c):
+            src32 = work.tile([P, PAIR, SLOTS * D], F32)
+            neigh32 = work.tile([P, PAIR, SLOTS * D], F32)
+            nc.vector.tensor_copy(out=src32[:], in_=xs_of[c][:])
+            for j in range(PAIR):
+                nc.vector.tensor_scalar(
+                    out=neigh32[:, j, :], in0=xn_of[c][:, j, :], scalar1=recip_of[c][:, j : j + 1], scalar2=None, op0=ALU.mult
+                )
+            wide_of[c] = (src32, neigh32)
 
-        def transpose_src(c):
-            words = xs_of[c][:].rearrange("p j f -> p (j f)").bitcast(F32)
+        def transpose_and_add(c):
             banks = []
-            for s in range(SLOTS):
-                bank = psum.tile([P, PAIR, 2, P], F32, tag="src_t%d" % s, name="src_t%d" % s)
-                for j in range(PAIR):
-                    for u in range(2):
-                        first = (j * SLOTS + s) * (D // 2) + u * P
-                        nc.tensor.transpose(bank[:, j, u, :], words[:, first : first + P], ident[:])
-                banks.append(bank)
-            src_t_of[c] = banks
-
-        def copy_first_src_slot(c):
-            first = work.tile([P, PAIR * D // 2], F32)
-            nc.scalar.copy(out=first[:], in_=src_t_of[c][0][:].rearrange("p j u n -> p (j u n)"))
-            first_of[c] = first
-
-        def sums(c):
-            xn = xn_of[c]
-            slot1 = src_t_of[c][1][:].rearrange("p j u n -> p (j u n)").bitcast(BF16)
-            slot2 = src_t_of[c][2][:].rearrange("p j u n -> p (j u n)").bitcast(BF16)
-            s01 = work.tile([P, PAIR * D], F32)
-            nsum = work.tile([P, PAIR, D], F32)
-            grouped = work.tile([P, PAIR * K], BF16, align_bytes=64, bufs=3)
-            nc.vector.tensor_tensor(out=s01[:], in0=first_of[c][:].bitcast(BF16), in1=slot1, op=ALU.add)
-            nc.vector.tensor_tensor(out=nsum[:], in0=n01_of[c][:], in1=xn[:, :, 2 * D : 3 * D], op=ALU.add)
-            grouped_v = grouped[:].rearrange("p (j g n u e) -> p j g n u e", j=PAIR, g=PASSES, u=2, e=2)
             for j in range(PAIR):
-                nc.vector.tensor_tensor(
-                    out=grouped_v[:, j, 0],
-                    in0=s01[:, j * D : (j + 1) * D].rearrange("p (u n e) -> p n u e", u=2, e=2),
-                    in1=slot2[:, j * D : (j + 1) * D].rearrange("p (u n e) -> p n u e", u=2, e=2),
-                    op=ALU.add,
-                )
-            nsum_of[c] = nsum
+                for g in range(PASSES):
+                    hid_t = psum.tile([P, 4, P], F32)
+                    for t in range(4):
+                        for s in range(SLOTS):
+                            first = s * D + t * P
+                            nc.tensor.matmul(
+                                out=hid_t[:, t, :],
+                                lhsT=wide_of[c][g][:, j, first : first + P],
+                                rhs=ident[:],
+                                is_transpose=True,
+                                start=(s == 0),
+                                stop=(s == SLOTS - 1),
+                            )
+                    banks.append(hid_t)
+            hid_t_of[c] = banks
+
+        def regroup(c):
+            grouped = work.tile([P, PAIR * K], BF16, align_bytes=64)
+            grouped_v = grouped[:].rearrange("p (b n t) -> p b n t", b=PAIR * PASSES, t=4)
+            for b in range(PAIR * PASSES):
+                nc.scalar.copy(out=grouped_v[:, b], in_=hid_t_of[c][b][:].rearrange("p t n -> p n t"))
             grouped_of[c] = grouped
-
-        def scale(c):
-            mean = work.tile([P, PAIR, D], BF16)
-            for j in range(PAIR):
-                nc.scalar.activation(
-                    out=mean[:, j, :], in_=nsum_of[c][:, j, :], func=ACT.Copy, scale=recip_of[c][:, j : j + 1]
-                )
-            mean_of[c] = mean
-
-        def transpose_mean(c):
-            words = mean_of[c][:].rearrange("p j k -> p (j k)").bitcast(F32)
-            mean_t = psum.tile([P, PAIR, 2, P], F32)
-            for j in range(PAIR):
-                for u in range(2):
-                    first = j * (D // 2) + u * P
-                    nc.tensor.transpose(mean_t[:, j, u, :], words[:, first : first + P], ident[:])
-            mean_t_of[c] = mean_t
-
-        def regroup_mean(c):
-            grouped_w = grouped_of[c][:].bitcast(F32).rearrange("p (j g n u) -> p j g n u", j=PAIR, g=PASSES, u=2)
-            nc.scalar.copy(out=grouped_w[:, :, 1], in_=mean_t_of[c][:].rearrange("p j u n -> p j n u"))
 
         def quantise_and_multiply(c):
             codes = work.tile([P, PAIR * PASSES * P], U32, align_bytes=64)
@@ -185,7 +153,7 @@ def tile_syntacticgcn_t_kernel(tc, src_node_features, neigh_node_features, W_map
             nc.vector.quantize_mx(out=codes[:].bitcast(FP8X4), scales=scales[:], in_=grouped_of[c][:])
             accs = []
             for j in range(PAIR):
-                acc = psum.tile([P, H], F32, bufs=4)
+                acc = psum.tile([P, H], F32)
                 for g in range(PASSES):
                     cols = slice((j * PASSES + g) * P, (j * PASSES + g + 1) * P)
                     nc.tensor.matmul_mx(
@@ -213,28 +181,20 @@ def tile_syntacticgcn_t_kernel(tc, src_node_features, neigh_node_features, W_map
 
         count(0)
         reciprocal_count(0)
-        add_first_two_neigh_slots(0)
-        transpose_src(0)
-        copy_first_src_slot(0)
         for i in range(N_PAIRS + 2):
             if i + PREFETCH < N_PAIRS:
                 load(i + PREFETCH)
             if i + 1 < N_PAIRS:
-                add_first_two_neigh_slots(i + 1)
                 count(i + 1)
             if i < N_PAIRS:
-                sums(i)
+                widen(i)
             if i + 1 < N_PAIRS:
-                transpose_src(i + 1)
-                copy_first_src_slot(i + 1)
                 reciprocal_count(i + 1)
             if 0 <= i - 1 < N_PAIRS:
-                regroup_mean(i - 1)
+                regroup(i - 1)
             if i < N_PAIRS:
-                scale(i)
+                transpose_and_add(i)
             if 0 <= i - 2:
                 finish(i - 2)
             if 0 <= i - 1 < N_PAIRS:
                 quantise_and_multiply(i - 1)
-            if i < N_PAIRS:
-                transpose_mean(i)

import concourse.mybir as mybir
from concourse.masks import make_identity

F32 = mybir.dt.float32
BF16 = mybir.dt.bfloat16
U32 = mybir.dt.uint32
U8 = mybir.dt.uint8
FP8X4 = mybir.dt.float8_e4m3fn_x4
ALU = mybir.AluOpType
ACT = mybir.ActivationFunctionType
AXIS = mybir.AxisListType

P = 128
SLOTS = 3
D = 512
H = 512
K = 2 * D
NODES = 4096
K_PASS = 512
PASSES = K // K_PASS
NODE_TILES = NODES // P
PAIR = 2
N_PAIRS = NODE_TILES // PAIR
PREFETCH = 3
SLOPE = 0.01

FLOPS = 2 * NODES * K * H


def tile_syntacticgcn_t_kernel(tc, src_node_features, neigh_node_features, W_map, b_map, out):
    nc = tc.nc

    src_v = src_node_features.rearrange("b (q t) m d -> (b q) t (m d)", t=NODE_TILES)
    neigh_v = neigh_node_features.rearrange("b (q t) m d -> (b q) t (m d)", t=NODE_TILES)
    out_v = out.rearrange("(p t) h -> p t h", t=NODE_TILES)

    with tc.tile_pool(name="const", bufs=1) as const, tc.tile_pool(name="data", bufs=PREFETCH + 1) as data, tc.tile_pool(
        name="work", bufs=2
    ) as work, tc.tile_pool(name="junk", bufs=4) as junk_pool, tc.psum_pool(name="psum", bufs=4) as psum:
        w_raw = const.tile([P, PASSES * 4 * H], BF16)
        nc.sync.dma_start(
            out=w_raw[:].rearrange("p (c h) -> p c h", c=4 * PASSES),
            in_=W_map.rearrange("(c p) h -> p c h", p=P),
        )
        ident = const.tile([P, P], F32)
        make_identity(nc, ident[:])

        xs_of = {}
        xn_of = {}

        def load(c):
            xn = data.tile([P, PAIR, SLOTS * D], BF16)
            nc.sync.dma_start(out=xn[:], in_=neigh_v[:, PAIR * c : PAIR * (c + 1), :])
            xs = data.tile([P, PAIR, SLOTS * D], BF16)
            nc.sync.dma_start(out=xs[:], in_=src_v[:, PAIR * c : PAIR * (c + 1), :])
            xn_of[c] = xn
            xs_of[c] = xs

        for c in range(PREFETCH):
            load(c)
        bias_bf = const.tile([P, H], BF16)
        nc.sync.dma_start(out=bias_bf[:], in_=b_map.partition_broadcast(P))

        w_grouped = const.tile([P, PASSES * H * 4], BF16, align_bytes=64)
        w_codes = const.tile([P, PASSES * H], U32, align_bytes=64)
        w_scales = const.tile([P, PASSES * H], U8, align_bytes=64)
        for g in range(PASSES):
            nc.vector.tensor_copy(
                out=w_grouped[:, g * 4 * H : (g + 1) * 4 * H].rearrange("p (h t) -> p h t", t=4),
                in_=w_raw[:, g * 4 * H : (g + 1) * 4 * H].rearrange("p (t h) -> p h t", t=4),
            )
        for g in range(PASSES):
            nc.vector.quantize_mx(
                out=w_codes[:, g * H : (g + 1) * H].bitcast(FP8X4),
                scales=w_scales[:, g * H : (g + 1) * H],
                in_=w_grouped[:, g * 4 * H : (g + 1) * 4 * H],
            )
        bias = const.tile([P, H], F32)
        nc.vector.tensor_copy(out=bias[:], in_=bias_bf[:])

        abs_sum_of = {}
        recip_of = {}
        wide_of = {}
        hid_t_of = {}
        grouped_of = {}
        acc_of = {}

        def count(c):
            abs_sum = work.tile([P, PAIR * SLOTS], F32)
            for j in range(PAIR):
                for s in range(SLOTS):
                    junk = junk_pool.tile([P, D], BF16)
                    nc.scalar.activation(
                        out=junk[:],
                        in_=xn_of[c][:, j, s * D : (s + 1) * D],
                        func=ACT.Abs,
                        accum_out=abs_sum[:, j * SLOTS + s : j * SLOTS + s + 1],
                    )
            abs_sum_of[c] = abs_sum

        def reciprocal_count(c):
            valid = work.tile([P, PAIR, SLOTS], F32)
            nc.vector.tensor_scalar(
                out=valid[:].rearrange("p j s -> p (j s)"), in0=abs_sum_of[c][:], scalar1=0.0, scalar2=None, op0=ALU.is_gt
            )
            num = work.tile([P, PAIR], F32)
            nc.vector.tensor_reduce(out=num[:], in_=valid[:], axis=AXIS.X, op=ALU.add)
            den = work.tile([P, PAIR], F32)
            nc.vector.tensor_scalar_max(den[:], num[:], 1.0)
            recip = work.tile([P, PAIR], F32)
            nc.vector.reciprocal(recip[:], den[:])
            recip_of[c] = recip

        def widen(c):
            src32 = work.tile([P, PAIR, SLOTS * D], F32)
            neigh32 = work.tile([P, PAIR, SLOTS * D], F32)
            nc.vector.tensor_copy(out=src32[:], in_=xs_of[c][:])
            for j in range(PAIR):
                nc.vector.tensor_scalar(
                    out=neigh32[:, j, :], in0=xn_of[c][:, j, :], scalar1=recip_of[c][:, j : j + 1], scalar2=None, op0=ALU.mult
                )
            wide_of[c] = (src32, neigh32)

        def transpose_and_add(c):
            banks = []
            for j in range(PAIR):
                for g in range(PASSES):
                    hid_t = psum.tile([P, 4, P], F32)
                    for t in range(4):
                        for s in range(SLOTS):
                            first = s * D + t * P
                            nc.tensor.matmul(
                                out=hid_t[:, t, :],
                                lhsT=wide_of[c][g][:, j, first : first + P],
                                rhs=ident[:],
                                is_transpose=True,
                                start=(s == 0),
                                stop=(s == SLOTS - 1),
                            )
                    banks.append(hid_t)
            hid_t_of[c] = banks

        def regroup(c):
            grouped = work.tile([P, PAIR * K], BF16, align_bytes=64)
            grouped_v = grouped[:].rearrange("p (b n t) -> p b n t", b=PAIR * PASSES, t=4)
            for b in range(PAIR * PASSES):
                nc.scalar.copy(out=grouped_v[:, b], in_=hid_t_of[c][b][:].rearrange("p t n -> p n t"))
            grouped_of[c] = grouped

        def quantise_and_multiply(c):
            codes = work.tile([P, PAIR * PASSES * P], U32, align_bytes=64)
            scales = work.tile([P, PAIR * PASSES * P], U8, align_bytes=64)
            nc.vector.quantize_mx(out=codes[:].bitcast(FP8X4), scales=scales[:], in_=grouped_of[c][:])
            accs = []
            for j in range(PAIR):
                acc = psum.tile([P, H], F32)
                for g in range(PASSES):
                    cols = slice((j * PASSES + g) * P, (j * PASSES + g + 1) * P)
                    nc.tensor.matmul_mx(
                        out=acc[:],
                        lhsT=codes[:, cols].bitcast(FP8X4),
                        lhsT_scale=scales[:, cols],
                        rhs=w_codes[:, g * H : (g + 1) * H].bitcast(FP8X4),
                        rhs_scale=w_scales[:, g * H : (g + 1) * H],
                        start=(g == 0),
                        stop=(g == PASSES - 1),
                    )
                accs.append(acc)
            acc_of[c] = accs

        def finish(c):
            biased = work.tile([P, PAIR, H], F32)
            result = work.tile([P, PAIR, H], F32)
            for j in range(PAIR):
                nc.vector.tensor_tensor(out=biased[:, j, :], in0=acc_of[c][j][:], in1=bias[:], op=ALU.add)
            for j in range(PAIR):
                nc.vector.scalar_tensor_tensor(
                    out=result[:, j, :], in0=biased[:, j, :], scalar=SLOPE, in1=biased[:, j, :], op0=ALU.mult, op1=ALU.max
                )
            nc.sync.dma_start(out=out_v[:, PAIR * c : PAIR * (c + 1), :], in_=result[:])

        count(0)
        reciprocal_count(0)
        for i in range(N_PAIRS + 2):
            if i + PREFETCH < N_PAIRS:
                load(i + PREFETCH)
            if i + 1 < N_PAIRS:
                count(i + 1)
            if i < N_PAIRS:
                widen(i)
            if i + 1 < N_PAIRS:
                reciprocal_count(i + 1)
            if 0 <= i - 1 < N_PAIRS:
                regroup(i - 1)
            if i < N_PAIRS:
                transpose_and_add(i)
            if 0 <= i - 2:
                finish(i - 2)
            if 0 <= i - 1 < N_PAIRS:
                quantise_and_multiply(i - 1)
